import numpy as np
import ml_dtypes


def mxq(x, axis, fmt="e4m3"):
    dtype, down = {"e4m3": (ml_dtypes.float8_e4m3fn, 7), "e5m2": (ml_dtypes.float8_e5m2, 14)}[fmt]
    v = np.moveaxis(np.asarray(x, np.float32).astype(ml_dtypes.bfloat16).astype(np.float64), axis, -1)
    blocks = v.reshape(v.shape[:-1] + (-1, 32))
    amax = np.abs(blocks).max(-1, keepdims=True)
    byte = np.maximum(np.where(amax > 0, np.frexp(amax)[1] - 1 + 127, 0) - down, 1)
    scale = np.exp2(byte - 127.0)
    codes = (blocks / scale).astype(np.float32).astype(dtype).astype(np.float64)
    return np.moveaxis((codes * scale).reshape(v.shape), -1, axis)


WIDE = False


def mx_kscale(k):
    if not WIDE:
        return np.ones(k)
    levels = np.array([10, -10, 5, -5, 0])
    a = np.random.permutation(np.resize(levels, k // 512 * 4)).reshape(k // 512, 4)
    idx = np.arange(k)
    return np.exp2(a[idx // 512, idx % 128 // 32])


BF16 = ml_dtypes.bfloat16


def bf(x):
    return np.asarray(x, np.float32).astype(BF16)


def f64(x):
    return np.asarray(x).astype(np.float64)


E2M1 = np.array([0.0, 0.5, 1.0, 1.5, 2.0, 3.0, 4.0, 6.0, -0.0, -0.5, -1.0, -1.5, -2.0, -3.0, -4.0, -6.0])


def pack_weight(w, fmt):
    k, n = w.shape
    w = f64(bf(w)).reshape(k // 32, 32, n)
    amax = np.abs(w).max(1)
    if fmt == "e4m3":
        byte = np.frexp(amax)[1] - 1 + 127 - 7
    else:
        mant, ex = np.frexp(amax / 6.0)
        byte = np.where(mant > 0.5, ex, ex - 1) + 127
    byte = np.clip(np.where(amax > 0, byte, 1), 1, 254)
    scaled = (w * np.exp2(127.0 - byte)[:, None, :]).reshape(k, n).astype(np.float32)
    by_word = np.ascontiguousarray(scaled.reshape(k // 512, 128, 4, n).transpose(0, 1, 3, 2))
    if fmt == "e4m3":
        words = by_word.astype(ml_dtypes.float8_e4m3fn).view(np.uint8)
    else:
        c = by_word.astype(ml_dtypes.float4_e2m1fn).view(np.uint8) & 0xF
        words = c[..., 0::2] | (c[..., 1::2] << 4)
    return np.ascontiguousarray(words), np.ascontiguousarray(byte.astype(np.uint8).reshape(k // 512, 16, n))


def unpack_weight(words, scales, fmt):
    g, p, n, _ = words.shape
    if fmt == "e4m3":
        vals = np.ascontiguousarray(words).view(ml_dtypes.float8_e4m3fn).astype(np.float64)
    else:
        nib = np.empty((g, p, n, 4), np.uint8)
        nib[..., 0::2] = words & 0xF
        nib[..., 1::2] = words >> 4
        vals = E2M1[nib]
    vals = vals * np.repeat(np.exp2(scales.astype(np.float64) - 127.0), 8, axis=1)[..., None]
    return vals.transpose(0, 1, 3, 2).reshape(g * 512, n)

def pack4(w):
    words, scales = pack_weight(w, "e2m1")
    return words.reshape(words.shape[0], 128, -1), scales


def unpack4(words, scales):
    return unpack_weight(words.reshape(words.shape[0], 128, -1, 2), scales, "e2m1")


B, S, D, E = 1, 1024, 768, 2
K = E * D


def setup_inputs():
    s = mx_kscale(K)
    att = bf(np.random.standard_normal((E, B, S, D)) * 0.3 * s.reshape(E, 1, 1, D))
    scene_reps = bf(np.random.standard_normal((B, S, D)))
    wo = np.random.standard_normal((D, K)) * 2.0 / np.sqrt(K) / s[None, :]
    words, scales = pack4(wo.T)
    return {"att": att,
            "scene_reps": scene_reps,
            "Wo_words": words,
            "Wo_scales": scales,
            "bo": bf(np.random.standard_normal(D) * 0.1),
            "gamma": bf(1.0 + np.random.standard_normal(D) * 0.1),
            "beta": bf(np.random.standard_normal(D) * 0.1)}


def reference(att, scene_reps, Wo_words, Wo_scales, bo, gamma, beta):
    cat = np.moveaxis(f64(att), 0, 2).reshape(B, S, K)
    fused = (mxq(cat, 2, "e4m3") @ unpack4(Wo_words, Wo_scales)) + f64(bo)
    y = f64(scene_reps) + fused
    mu = y.mean(-1, keepdims=True)
    var = y.var(-1, keepdims=True)
    return (y - mu) / np.sqrt(var + 1e-5) * f64(gamma) + f64(beta)

@@ -1,0 +1,202 @@
+from contextlib import ExitStack
+
+import concourse.mybir as mybir
+from concourse.masks import make_identity
+
+F32 = mybir.dt.float32
+BF16 = mybir.dt.bfloat16
+I32 = mybir.dt.int32
+U32 = mybir.dt.uint32
+U8 = mybir.dt.uint8
+FP8X4 = mybir.dt.float8_e4m3fn_x4
+FP4X4 = mybir.dt.float4_e2m1fn_x4
+ALU = mybir.AluOpType
+ACT = mybir.ActivationFunctionType
+
+P = 128
+S = 1024
+D = 768
+E = 2
+K = E * D
+K_PASS = 4 * P
+PASSES = K // K_PASS
+TILES = S // P
+PAIRS = TILES // 2
+N_WIDE = 512
+N_NARROW = 128
+EPS = 1e-5
+
+FLOPS = 2 * S * K * D
+
+
+def tile_heterogeneousgraphtransformer_pb_kernel(
+    tc, att, scene_reps, Wo_words, Wo_scales, bo, gamma, beta, out
+):
+    nc = tc.nc
+
+    att_v = att.rearrange("e b (p j) d -> e p (b j) d", j=TILES)
+    scene_v = scene_reps.rearrange("b (p j) d -> p (b j) d", j=TILES)
+    out_v = out.rearrange("b (p j) d -> p (b j) d", j=TILES)
+
+    with ExitStack() as ctx:
+        consts = ctx.enter_context(tc.tile_pool(name="consts", bufs=1))
+        inputs = ctx.enter_context(tc.tile_pool(name="inputs", bufs=1))
+        stage = ctx.enter_context(tc.tile_pool(name="stage", bufs=3))
+        work = ctx.enter_context(tc.tile_pool(name="work", bufs=3))
+        small = ctx.enter_context(tc.tile_pool(name="small", bufs=4))
+        psum_t = ctx.enter_context(tc.psum_pool(name="psum_t", bufs=3))
+        psum_acc = ctx.enter_context(tc.psum_pool(name="psum_acc", bufs=2))
+        psum_c = ctx.enter_context(tc.psum_pool(name="psum_c", bufs=1))
+
+        eps = consts.tile([P, 1], F32)
+        nc.vector.memset(eps[:], EPS)
+        warm = consts.tile([P, 1], F32)
+        nc.scalar.activation(out=warm[:], in_=eps[:], func=ACT.Sqrt)
+        ident = consts.tile([P, P], F32)
+        make_identity(nc, ident[:])
+        ones = consts.tile([P, P], BF16)
+        nc.vector.memset(ones[:], 1.0)
+        rows = consts.tile([P, 3, D], BF16)
+        nc.vector.memset(rows[:], 0.0)
+        w_planes = consts.tile([P, PASSES, D], U8, align_bytes=64)
+        nc.vector.memset(w_planes[:].bitcast(I32), 0)
+
+        cat = [inputs.tile([P, 2, E, D], BF16, name="cat%d" % q) for q in range(PAIRS)]
+        scene = [inputs.tile([P, 2, D], BF16, name="scene%d" % q) for q in range(PAIRS)]
+        w_words = consts.tile([P, PASSES, 2 * D], U8, align_bytes=64)
+
+        def load_pair(q):
+            for e in range(E):
+                nc.sync.dma_start(out=cat[q][:, :, e, :], in_=att_v[e, :, 2 * q : 2 * q + 2, :])
+            nc.sync.dma_start(out=scene[q][:], in_=scene_v[:, 2 * q : 2 * q + 2, :])
+
+        for e in range(E):
+            nc.sync.dma_start(out=cat[0][:, :, e, :], in_=att_v[e, :, 0:2, :])
+        for r in range(4):
+            nc.sync.dma_start(
+                out=w_planes[r:P:32].bitcast(I32),
+                in_=Wo_scales.bitcast(I32)[:, r:16:4, :].rearrange("g q n -> q g n"),
+            )
+        nc.sync.dma_start(
+            out=w_words[:].bitcast(I32), in_=Wo_words.bitcast(I32).rearrange("g p n -> p g n")
+        )
+        for i, vec in enumerate((bo, gamma, beta)):
+            nc.sync.dma_start(out=rows[0:1, i, :], in_=vec.unsqueeze(0))
+        nc.sync.dma_start(out=scene[0][:], in_=scene_v[:, 0:2, :])
+        for q in range(1, PAIRS):
+            load_pair(q)
+
+        spread = consts.tile([P, 3, D], BF16)
+        for i in range(3):
+            for h in range(2):
+                half = slice(h * (D // 2), (h + 1) * (D // 2))
+                bc = psum_c.tile([P, D // 2], F32)
+                nc.tensor.matmul(out=bc[:], lhsT=ones[:], rhs=rows[:, i, half], start=True, stop=True)
+                nc.scalar.copy(out=spread[:, i, half], in_=bc[:])
+        bo_all = spread[:, 0, :]
+        gamma_all = spread[:, 1, :]
+        beta_all = spread[:, 2, :]
+
+        codes = [inputs.tile([P, PASSES, 2 * P], U32, name="codes%d" % q, align_bytes=64) for q in range(PAIRS)]
+        planes = [inputs.tile([P, PASSES, 2 * P], U8, name="planes%d" % q, align_bytes=64) for q in range(PAIRS)]
+        resid = [inputs.tile([P, 2, D], F32, name="resid%d" % q) for q in range(PAIRS)]
+
+        def transpose_and_quantise(q):
+            for g in range(PASSES):
+                xt = psum_t.tile([P, 2, 2, P], F32)
+                for jj in range(2):
+                    words = cat[q][:, jj].rearrange("p e d -> p (e d)").bitcast(F32)
+                    for u in range(2):
+                        nc.tensor.transpose(
+                            out=xt[:, jj, u, :],
+                            in_=words[:, 2 * P * g + u : 2 * P * (g + 1) : 2],
+                            identity=ident[:],
+                        )
+                grouped = stage.tile([P, 2, P, 4], BF16, align_bytes=64)
+                nc.scalar.copy(
+                    out=grouped[:].bitcast(F32),
+                    in_=xt[:].rearrange("p j u r -> p j r u"),
+                )
+                nc.vector.quantize_mx(
+                    out=codes[q][:, g, :].bitcast(FP8X4),
+                    scales=planes[q][:, g, :],
+                    in_=grouped[:].rearrange("p j r t -> p (j r t)"),
+                )
+
+        def add_bias_to_residual(q):
+            for jj in range(2):
+                nc.gpsimd.tensor_tensor(
+                    out=resid[q][:, jj, :], in0=scene[q][:, jj, :], in1=bo_all, op=ALU.add
+                )
+
+        def project(j):
+            q, jj = divmod(j, 2)
+            tokens = slice(jj * P, (jj + 1) * P)
+
+            def mx_group(acc, n0, n):
+                for g in range(PASSES):
+                    nc.tensor.matmul_mx(
+                        out=acc,
+                        lhsT=codes[q][:, g, tokens].bitcast(FP8X4),
+                        lhsT_scale=planes[q][:, g, tokens],
+                        rhs=w_words[:, g, 2 * n0 : 2 * (n0 + n)].bitcast(FP4X4),
+                        rhs_scale=w_planes[:, g, n0 : n0 + n],
+                        start=(g == 0),
+                        stop=(g == PASSES - 1),
+                    )
+
+            acc_wide = psum_acc.tile([P, N_WIDE], F32)
+            acc_rest = psum_acc.tile([P, D - N_WIDE], F32)
+            mx_group(acc_wide[:], 0, N_WIDE)
+            for n0 in range(N_WIDE, D, N_NARROW):
+                mx_group(acc_rest[:, n0 - N_WIDE : n0 - N_WIDE + N_NARROW], n0, N_NARROW)
+
+            y = work.tile([P, D], F32)
+            sums = small.tile([P, 2], F32)
+            nc.vector.scalar_tensor_tensor(
+                out=y[:, 0:N_WIDE], in0=acc_wide[:], scalar=1.0, in1=resid[q][:, jj, 0:N_WIDE],
+                op0=ALU.mult, op1=ALU.add, accum_out=sums[:, 0:1],
+            )
+            nc.vector.scalar_tensor_tensor(
+                out=y[:, N_WIDE:D], in0=acc_rest[:], scalar=1.0, in1=resid[q][:, jj, N_WIDE:D],
+                op0=ALU.mult, op1=ALU.add, accum_out=sums[:, 1:2],
+            )
+            return y, sums
+
+        def normalise(j, y, sums):
+            neg_mean = small.tile([P, 1], F32)
+            nc.vector.tensor_scalar(
+                out=neg_mean[:], in0=sums[:, 0:1], scalar1=sums[:, 1:2], scalar2=-1.0 / D,
+                op0=ALU.add, op1=ALU.mult,
+            )
+            squares = work.tile([P, D], F32)
+            ssq = small.tile([P, 1], F32)
+            nc.scalar.activation(
+                out=squares[:], in_=y[:], func=ACT.Square, bias=neg_mean[:], scale=1.0, accum_out=ssq[:]
+            )
+            centred = work.tile([P, D], F32)
+            nc.vector.scalar_tensor_tensor(
+                out=centred[:], in0=y[:], scalar=neg_mean[:], in1=gamma_all, op0=ALU.add, op1=ALU.mult
+            )
+            std = small.tile([P, 1], F32)
+            nc.scalar.activation(out=std[:], in_=ssq[:], func=ACT.Sqrt, bias=eps[:], scale=1.0 / D)
+            rstd = small.tile([P, 1], F32)
+            nc.vector.reciprocal(out=rstd[:], in_=std[:])
+            result = work.tile([P, D], F32)
+            nc.vector.scalar_tensor_tensor(
+                out=result[:], in0=centred[:], scalar=rstd[:], in1=beta_all, op0=ALU.mult, op1=ALU.add
+            )
+            nc.sync.dma_start(out=out_v[:, j, :], in_=result[:])
+
+        transpose_and_quantise(0)
+        add_bias_to_residual(0)
+        transpose_and_quantise(1)
+        for q in range(PAIRS):
+            first = project(2 * q)
+            second = project(2 * q + 1)
+            if q + 1 < PAIRS:
+                add_bias_to_residual(q + 1)
+            if q + 2 < PAIRS:
+                transpose_and_quantise(q + 2)
+            normalise(2 * q, *first)
+            normalise(2 * q + 1, *second)

@@ -21,7 +21,6 @@ K = E * D
 K_PASS = 4 * P
 PASSES = K // K_PASS
 TILES = S // P
-PAIRS = TILES // 2
 N_WIDE = 512
 N_NARROW = 128
 EPS = 1e-5
@@ -34,44 +33,42 @@ def tile_heterogeneousgraphtransformer_pb_kernel(
 ):
     nc = tc.nc
 
-    att_v = att.rearrange("e b (p j) d -> e p (b j) d", j=TILES)
-    scene_v = scene_reps.rearrange("b (p j) d -> p (b j) d", j=TILES)
-    out_v = out.rearrange("b (p j) d -> p (b j) d", j=TILES)
+    att_v = att.rearrange("e b (p j) d -> (b j) p e d", j=TILES)
+    scene_v = scene_reps.rearrange("b (p j) d -> (b j) p d", j=TILES)
+    out_v = out.rearrange("b (p j) d -> (b j) p d", j=TILES)
 
     with ExitStack() as ctx:
         consts = ctx.enter_context(tc.tile_pool(name="consts", bufs=1))
         inputs = ctx.enter_context(tc.tile_pool(name="inputs", bufs=1))
-        stage = ctx.enter_context(tc.tile_pool(name="stage", bufs=3))
+        stage = ctx.enter_context(tc.tile_pool(name="stage", bufs=9))
         work = ctx.enter_context(tc.tile_pool(name="work", bufs=3))
         small = ctx.enter_context(tc.tile_pool(name="small", bufs=4))
         psum_t = ctx.enter_context(tc.psum_pool(name="psum_t", bufs=3))
         psum_acc = ctx.enter_context(tc.psum_pool(name="psum_acc", bufs=2))
         psum_c = ctx.enter_context(tc.psum_pool(name="psum_c", bufs=1))
+        ctx.enter_context(tc.manual_schedule())
 
+        rows = consts.tile([P, 3, D], BF16)
+        nc.vector.memset(rows[:, 0, :].bitcast(I32), 0)
+        w_planes = consts.tile([P, PASSES, D], U8, align_bytes=64)
+        nc.vector.memset(w_planes[:].bitcast(I32), 0)
+        nc.vector.memset(rows[:, 1:3, :].bitcast(I32), 0)
         eps = consts.tile([P, 1], F32)
         nc.vector.memset(eps[:], EPS)
+        ones = consts.tile([P, P], BF16)
+        nc.vector.memset(ones[:], 1.0)
         warm = consts.tile([P, 1], F32)
         nc.scalar.activation(out=warm[:], in_=eps[:], func=ACT.Sqrt)
         ident = consts.tile([P, P], F32)
         make_identity(nc, ident[:])
-        ones = consts.tile([P, P], BF16)
-        nc.vector.memset(ones[:], 1.0)
-        rows = consts.tile([P, 3, D], BF16)
-        nc.vector.memset(rows[:], 0.0)
-        w_planes = consts.tile([P, PASSES, D], U8, align_bytes=64)
-        nc.vector.memset(w_planes[:].bitcast(I32), 0)
 
-        cat = [inputs.tile([P, 2, E, D], BF16, name="cat%d" % q) for q in range(PAIRS)]
-        scene = [inputs.tile([P, 2, D], BF16, name="scene%d" % q) for q in range(PAIRS)]
+        cat = [inputs.tile([P, E, D], BF16, name="cat%d" % j) for j in range(TILES)]
+        scene = [inputs.tile([P, D], BF16, name="scene%d" % j) for j in range(TILES)]
         w_words = consts.tile([P, PASSES, 2 * D], U8, align_bytes=64)
 
-        def load_pair(q):
-            for e in range(E):
-                nc.sync.dma_start(out=cat[q][:, :, e, :], in_=att_v[e, :, 2 * q : 2 * q + 2, :])
-            nc.sync.dma_start(out=scene[q][:], in_=scene_v[:, 2 * q : 2 * q + 2, :])
-
-        for e in range(E):
-            nc.sync.dma_start(out=cat[0][:, :, e, :], in_=att_v[e, :, 0:2, :])
+        nc.sync.dma_start(out=cat[0][:], in_=att_v[0])
+        nc.sync.dma_start(out=rows[0:1, 0, :], in_=bo.unsqueeze(0))
+        nc.sync.dma_start(out=scene[0][:], in_=scene_v[0])
         for r in range(4):
             nc.sync.dma_start(
                 out=w_planes[r:P:32].bitcast(I32),
@@ -80,65 +77,58 @@ def tile_heterogeneousgraphtransformer_pb_kernel(
         nc.sync.dma_start(
             out=w_words[:].bitcast(I32), in_=Wo_words.bitcast(I32).rearrange("g p n -> p g n")
         )
-        for i, vec in enumerate((bo, gamma, beta)):
-            nc.sync.dma_start(out=rows[0:1, i, :], in_=vec.unsqueeze(0))
-        nc.sync.dma_start(out=scene[0][:], in_=scene_v[:, 0:2, :])
-        for q in range(1, PAIRS):
-            load_pair(q)
+        nc.sync.dma_start(out=rows[0:1, 1, :], in_=gamma.unsqueeze(0))
+        nc.sync.dma_start(out=rows[0:1, 2, :], in_=beta.unsqueeze(0))
+        for j in range(1, TILES):
+            nc.sync.dma_start(out=cat[j][:], in_=att_v[j])
+            nc.sync.dma_start(out=scene[j][:], in_=scene_v[j])
 
+        codes = [inputs.tile([P, PASSES, P], U32, name="codes%d" % j, align_bytes=64) for j in range(TILES)]
+        planes = [inputs.tile([P, PASSES, P], U8, name="planes%d" % j, align_bytes=64) for j in range(TILES)]
+        resid = [inputs.tile([P, D], F32, name="resid%d" % j) for j in range(TILES)]
         spread = consts.tile([P, 3, D], BF16)
-        for i in range(3):
+        bo_all = spread[:, 0, :]
+        gamma_all = spread[:, 1, :]
+        beta_all = spread[:, 2, :]
+
+        def spread_vector(i):
             for h in range(2):
                 half = slice(h * (D // 2), (h + 1) * (D // 2))
                 bc = psum_c.tile([P, D // 2], F32)
                 nc.tensor.matmul(out=bc[:], lhsT=ones[:], rhs=rows[:, i, half], start=True, stop=True)
                 nc.scalar.copy(out=spread[:, i, half], in_=bc[:])
-        bo_all = spread[:, 0, :]
-        gamma_all = spread[:, 1, :]
-        beta_all = spread[:, 2, :]
 
-        codes = [inputs.tile([P, PASSES, 2 * P], U32, name="codes%d" % q, align_bytes=64) for q in range(PAIRS)]
-        planes = [inputs.tile([P, PASSES, 2 * P], U8, name="planes%d" % q, align_bytes=64) for q in range(PAIRS)]
-        resid = [inputs.tile([P, 2, D], F32, name="resid%d" % q) for q in range(PAIRS)]
-
-        def transpose_and_quantise(q):
+        def transpose(j):
+            words = cat[j][:].rearrange("p e d -> p (e d)").bitcast(F32)
+            grouped = []
             for g in range(PASSES):
-                xt = psum_t.tile([P, 2, 2, P], F32)
-                for jj in range(2):
-                    words = cat[q][:, jj].rearrange("p e d -> p (e d)").bitcast(F32)
-                    for u in range(2):
-                        nc.tensor.transpose(
-                            out=xt[:, jj, u, :],
-                            in_=words[:, 2 * P * g + u : 2 * P * (g + 1) : 2],
-                            identity=ident[:],
-                        )
-                grouped = stage.tile([P, 2, P, 4], BF16, align_bytes=64)
-                nc.scalar.copy(
-                    out=grouped[:].bitcast(F32),
-                    in_=xt[:].rearrange("p j u r -> p j r u"),
-                )
-                nc.vector.quantize_mx(
-                    out=codes[q][:, g, :].bitcast(FP8X4),
-                    scales=planes[q][:, g, :],
-                    in_=grouped[:].rearrange("p j r t -> p (j r t)"),
-                )
+                xt = psum_t.tile([P, 2, P], F32)
+                for u in range(2):
+                    nc.tensor.transpose(
+                        out=xt[:, u, :],
+                        in_=words[:, 2 * P * g + u : 2 * P * (g + 1) : 2],
+                        identity=ident[:],
+                    )
+                side_by_side = stage.tile([P, P, 4], BF16, align_bytes=64)
+                nc.scalar.copy(out=side_by_side[:].bitcast(F32), in_=xt[:].rearrange("p u r -> p r u"))
+                grouped.append(side_by_side)
+            return grouped
 
-        def add_bias_to_residual(q):
-            for jj in range(2):
-                nc.gpsimd.tensor_tensor(
-                    out=resid[q][:, jj, :], in0=scene[q][:, jj, :], in1=bo_all, op=ALU.add
+        def quantise(j, grouped):
+            for g in range(PASSES):
+                nc.vector.quantize_mx(
+                    out=codes[j][:, g, :].bitcast(FP8X4),
+                    scales=planes[j][:, g, :],
+                    in_=grouped[g][:].rearrange("p r t -> p (r t)"),
                 )
 
         def project(j):
-            q, jj = divmod(j, 2)
-            tokens = slice(jj * P, (jj + 1) * P)
-
             def mx_group(acc, n0, n):
                 for g in range(PASSES):
                     nc.tensor.matmul_mx(
                         out=acc,
-                        lhsT=codes[q][:, g, tokens].bitcast(FP8X4),
-                        lhsT_scale=planes[q][:, g, tokens],
+                        lhsT=codes[j][:, g, :].bitcast(FP8X4),
+                        lhsT_scale=planes[j][:, g, :],
                         rhs=w_words[:, g, 2 * n0 : 2 * (n0 + n)].bitcast(FP4X4),
                         rhs_scale=w_planes[:, g, n0 : n0 + n],
                         start=(g == 0),
@@ -150,53 +140,80 @@ def tile_heterogeneousgraphtransformer_pb_kernel(
             mx_group(acc_wide[:], 0, N_WIDE)
             for n0 in range(N_WIDE, D, N_NARROW):
                 mx_group(acc_rest[:, n0 - N_WIDE : n0 - N_WIDE + N_NARROW], n0, N_NARROW)
+            return acc_wide, acc_rest
 
+        def add_residual(j, acc_wide, acc_rest):
             y = work.tile([P, D], F32)
             sums = small.tile([P, 2], F32)
             nc.vector.scalar_tensor_tensor(
-                out=y[:, 0:N_WIDE], in0=acc_wide[:], scalar=1.0, in1=resid[q][:, jj, 0:N_WIDE],
+                out=y[:, 0:N_WIDE], in0=acc_wide[:], scalar=1.0, in1=resid[j][:, 0:N_WIDE],
                 op0=ALU.mult, op1=ALU.add, accum_out=sums[:, 0:1],
             )
             nc.vector.scalar_tensor_tensor(
-                out=y[:, N_WIDE:D], in0=acc_rest[:], scalar=1.0, in1=resid[q][:, jj, N_WIDE:D],
+                out=y[:, N_WIDE:D], in0=acc_rest[:], scalar=1.0, in1=resid[j][:, N_WIDE:D],
                 op0=ALU.mult, op1=ALU.add, accum_out=sums[:, 1:2],
             )
             return y, sums
 
-        def normalise(j, y, sums):
+        def negative_mean(sums):
             neg_mean = small.tile([P, 1], F32)
             nc.vector.tensor_scalar(
                 out=neg_mean[:], in0=sums[:, 0:1], scalar1=sums[:, 1:2], scalar2=-1.0 / D,
                 op0=ALU.add, op1=ALU.mult,
             )
+            return neg_mean
+
+        def standard_deviation(y, neg_mean):
             squares = work.tile([P, D], F32)
             ssq = small.tile([P, 1], F32)
             nc.scalar.activation(
                 out=squares[:], in_=y[:], func=ACT.Square, bias=neg_mean[:], scale=1.0, accum_out=ssq[:]
             )
+            std = small.tile([P, 1], F32)
+            nc.scalar.activation(out=std[:], in_=ssq[:], func=ACT.Sqrt, bias=eps[:], scale=1.0 / D)
+            return std
+
+        def centre_and_gain(y, neg_mean):
             centred = work.tile([P, D], F32)
             nc.vector.scalar_tensor_tensor(
                 out=centred[:], in0=y[:], scalar=neg_mean[:], in1=gamma_all, op0=ALU.add, op1=ALU.mult
             )
-            std = small.tile([P, 1], F32)
-            nc.scalar.activation(out=std[:], in_=ssq[:], func=ACT.Sqrt, bias=eps[:], scale=1.0 / D)
-            rstd = small.tile([P, 1], F32)
-            nc.vector.reciprocal(out=rstd[:], in_=std[:])
+            return centred
+
+        def scale_shift_store(j, centred, rstd):
             result = work.tile([P, D], F32)
             nc.vector.scalar_tensor_tensor(
                 out=result[:], in0=centred[:], scalar=rstd[:], in1=beta_all, op0=ALU.mult, op1=ALU.add
             )
-            nc.sync.dma_start(out=out_v[:, j, :], in_=result[:])
+            nc.sync.dma_start(out=out_v[j], in_=result[:])
 
-        transpose_and_quantise(0)
-        add_bias_to_residual(0)
-        transpose_and_quantise(1)
-        for q in range(PAIRS):
-            first = project(2 * q)
-            second = project(2 * q + 1)
-            if q + 1 < PAIRS:
-                add_bias_to_residual(q + 1)
-            if q + 2 < PAIRS:
-                transpose_and_quantise(q + 2)
-            normalise(2 * q, *first)
-            normalise(2 * q + 1, *second)
+        grouped = {0: transpose(0)}
+        spread_vector(0)
+        quantise(0, grouped[0])
+        nc.vector.tensor_tensor(out=resid[0][:], in0=scene[0][:], in1=bo_all, op=ALU.add)
+        for j in range(1, TILES):
+            nc.gpsimd.tensor_tensor(out=resid[j][:], in0=scene[j][:], in1=bo_all, op=ALU.add)
+        acc = project(0)
+        grouped[1] = transpose(1)
+        spread_vector(1)
+        spread_vector(2)
+
+        previous = None
+        for j in range(TILES + 1):
+            if j < TILES:
+                y, sums = add_residual(j, *acc)
+            if previous is not None:
+                rstd = small.tile([P, 1], F32)
+                nc.vector.reciprocal(out=rstd[:], in_=previous[1][:])
+            if j < TILES:
+                neg_mean = negative_mean(sums)
+                std = standard_deviation(y, neg_mean)
+            if j + 2 < TILES:
+                grouped[j + 2] = transpose(j + 2)
+            if j + 1 < TILES:
+                quantise(j + 1, grouped[j + 1])
+                acc = project(j + 1)
+            if previous is not None:
+                scale_shift_store(j - 1, previous[0], rstd)
+            if j < TILES:
+                previous = (centre_and_gain(y, neg_mean), std)

@@ -44,7 +44,7 @@ def tile_heterogeneousgraphtransformer_pb_kernel(
         work = ctx.enter_context(tc.tile_pool(name="work", bufs=3))
         small = ctx.enter_context(tc.tile_pool(name="small", bufs=4))
         psum_t = ctx.enter_context(tc.psum_pool(name="psum_t", bufs=3))
-        psum_acc = ctx.enter_context(tc.psum_pool(name="psum_acc", bufs=2))
+        psum_acc = ctx.enter_context(tc.psum_pool(name="psum_acc", bufs=1))
         psum_c = ctx.enter_context(tc.psum_pool(name="psum_c", bufs=1))
         ctx.enter_context(tc.manual_schedule())
 
@@ -86,17 +86,17 @@ def tile_heterogeneousgraphtransformer_pb_kernel(
         codes = [inputs.tile([P, PASSES, P], U32, name="codes%d" % j, align_bytes=64) for j in range(TILES)]
         planes = [inputs.tile([P, PASSES, P], U8, name="planes%d" % j, align_bytes=64) for j in range(TILES)]
         resid = [inputs.tile([P, D], F32, name="resid%d" % j) for j in range(TILES)]
-        spread = consts.tile([P, 3, D], BF16)
-        bo_all = spread[:, 0, :]
-        gamma_all = spread[:, 1, :]
-        beta_all = spread[:, 2, :]
+        bo_psum = psum_c.tile([P, D], BF16)
+        gamma_psum = psum_c.tile([P, D], BF16)
+        beta_psum = psum_c.tile([P, D], BF16)
+        bo_sbuf = consts.tile([P, D], BF16)
 
-        def spread_vector(i):
+        def spread_vector(i, everywhere):
             for h in range(2):
                 half = slice(h * (D // 2), (h + 1) * (D // 2))
-                bc = psum_c.tile([P, D // 2], F32)
-                nc.tensor.matmul(out=bc[:], lhsT=ones[:], rhs=rows[:, i, half], start=True, stop=True)
-                nc.scalar.copy(out=spread[:, i, half], in_=bc[:])
+                nc.tensor.matmul(
+                    out=everywhere[:, half], lhsT=ones[:], rhs=rows[:, i, half], start=True, stop=True
+                )
 
         def transpose(j):
             words = cat[j][:].rearrange("p e d -> p (e d)").bitcast(F32)
@@ -176,27 +176,28 @@ def tile_heterogeneousgraphtransformer_pb_kernel(
         def centre_and_gain(y, neg_mean):
             centred = work.tile([P, D], F32)
             nc.vector.scalar_tensor_tensor(
-                out=centred[:], in0=y[:], scalar=neg_mean[:], in1=gamma_all, op0=ALU.add, op1=ALU.mult
+                out=centred[:], in0=y[:], scalar=neg_mean[:], in1=gamma_psum[:], op0=ALU.add, op1=ALU.mult
             )
             return centred
 
         def scale_shift_store(j, centred, rstd):
             result = work.tile([P, D], F32)
             nc.vector.scalar_tensor_tensor(
-                out=result[:], in0=centred[:], scalar=rstd[:], in1=beta_all, op0=ALU.mult, op1=ALU.add
+                out=result[:], in0=centred[:], scalar=rstd[:], in1=beta_psum[:], op0=ALU.mult, op1=ALU.add
             )
             nc.sync.dma_start(out=out_v[j], in_=result[:])
 
         grouped = {0: transpose(0)}
-        spread_vector(0)
+        spread_vector(0, bo_psum)
+        nc.scalar.copy(out=bo_sbuf[:], in_=bo_psum[:])
         quantise(0, grouped[0])
-        nc.vector.tensor_tensor(out=resid[0][:], in0=scene[0][:], in1=bo_all, op=ALU.add)
+        nc.vector.tensor_tensor(out=resid[0][:], in0=scene[0][:], in1=bo_psum[:], op=ALU.add)
         for j in range(1, TILES):
-            nc.gpsimd.tensor_tensor(out=resid[j][:], in0=scene[j][:], in1=bo_all, op=ALU.add)
+            nc.gpsimd.tensor_tensor(out=resid[j][:], in0=scene[j][:], in1=bo_sbuf[:], op=ALU.add)
         acc = project(0)
         grouped[1] = transpose(1)
-        spread_vector(1)
-        spread_vector(2)
+        spread_vector(1, gamma_psum)
+        spread_vector(2, beta_psum)
 
         previous = None
         for j in range(TILES + 1):

@@ -58,7 +58,7 @@ def tile_heterogeneousgraphtransformer_pb_kernel(
         ones = consts.tile([P, P], BF16)
         nc.vector.memset(ones[:], 1.0)
         warm = consts.tile([P, 1], F32)
-        nc.scalar.activation(out=warm[:], in_=eps[:], func=ACT.Sqrt)
+        nc.scalar.activation(out=warm[:], in_=eps[:], func=ACT.Abs_reciprocal_sqrt)
         ident = consts.tile([P, P], F32)
         make_identity(nc, ident[:])
 
@@ -155,23 +155,22 @@ def tile_heterogeneousgraphtransformer_pb_kernel(
             )
             return y, sums
 
-        def negative_mean(sums):
+        def statistics(y, sums):
+            parts = small.tile([P, 2], F32)
             neg_mean = small.tile([P, 1], F32)
-            nc.vector.tensor_scalar(
-                out=neg_mean[:], in0=sums[:, 0:1], scalar1=sums[:, 1:2], scalar2=-1.0 / D,
-                op0=ALU.add, op1=ALU.mult,
+            nc.scalar.activation(
+                out=parts[:], in_=sums[:], func=ACT.Copy, scale=-1.0 / D, accum_out=neg_mean[:]
             )
-            return neg_mean
-
-        def standard_deviation(y, neg_mean):
             squares = work.tile([P, D], F32)
             ssq = small.tile([P, 1], F32)
             nc.scalar.activation(
                 out=squares[:], in_=y[:], func=ACT.Square, bias=neg_mean[:], scale=1.0, accum_out=ssq[:]
             )
-            std = small.tile([P, 1], F32)
-            nc.scalar.activation(out=std[:], in_=ssq[:], func=ACT.Sqrt, bias=eps[:], scale=1.0 / D)
-            return std
+            rstd = small.tile([P, 1], F32)
+            nc.scalar.activation(
+                out=rstd[:], in_=ssq[:], func=ACT.Abs_reciprocal_sqrt, bias=eps[:], scale=1.0 / D
+            )
+            return neg_mean, rstd
 
         def centre_and_gain(y, neg_mean):
             centred = work.tile([P, D], F32)
@@ -203,18 +202,13 @@ def tile_heterogeneousgraphtransformer_pb_kernel(
         for j in range(TILES + 1):
             if j < TILES:
                 y, sums = add_residual(j, *acc)
-            if previous is not None:
-                rstd = small.tile([P, 1], F32)
-                nc.vector.reciprocal(out=rstd[:], in_=previous[1][:])
-            if j < TILES:
-                neg_mean = negative_mean(sums)
-                std = standard_deviation(y, neg_mean)
+                neg_mean, rstd = statistics(y, sums)
             if j + 2 < TILES:
                 grouped[j + 2] = transpose(j + 2)
             if j + 1 < TILES:
                 quantise(j + 1, grouped[j + 1])
                 acc = project(j + 1)
             if previous is not None:
-                scale_shift_store(j - 1, previous[0], rstd)
+                scale_shift_store(j - 1, *previous)
             if j < TILES:
-                previous = (centre_and_gain(y, neg_mean), std)
+                previous = (centre_and_gain(y, neg_mean), rstd)

@@ -23,6 +23,8 @@ PASSES = K // K_PASS
 TILES = S // P
 N_WIDE = 512
 N_NARROW = 128
+RESID_PIECE = 256
+AHEAD = 2
 EPS = 1e-5
 
 FLOPS = 2 * S * K * D
@@ -40,11 +42,11 @@ def tile_heterogeneousgraphtransformer_pb_kernel(
     with ExitStack() as ctx:
         consts = ctx.enter_context(tc.tile_pool(name="consts", bufs=1))
         inputs = ctx.enter_context(tc.tile_pool(name="inputs", bufs=1))
-        stage = ctx.enter_context(tc.tile_pool(name="stage", bufs=9))
+        stage = ctx.enter_context(tc.tile_pool(name="stage", bufs=12))
         work = ctx.enter_context(tc.tile_pool(name="work", bufs=3))
         small = ctx.enter_context(tc.tile_pool(name="small", bufs=4))
         psum_t = ctx.enter_context(tc.psum_pool(name="psum_t", bufs=3))
-        psum_acc = ctx.enter_context(tc.psum_pool(name="psum_acc", bufs=1))
+        psum_acc = ctx.enter_context(tc.psum_pool(name="psum_acc", bufs=2))
         psum_c = ctx.enter_context(tc.psum_pool(name="psum_c", bufs=1))
         ctx.enter_context(tc.manual_schedule())
 
@@ -86,7 +88,7 @@ def tile_heterogeneousgraphtransformer_pb_kernel(
         codes = [inputs.tile([P, PASSES, P], U32, name="codes%d" % j, align_bytes=64) for j in range(TILES)]
         planes = [inputs.tile([P, PASSES, P], U8, name="planes%d" % j, align_bytes=64) for j in range(TILES)]
         resid = [inputs.tile([P, D], F32, name="resid%d" % j) for j in range(TILES)]
-        bo_psum = psum_c.tile([P, D], BF16)
+        bo_psum = psum_t.tile([P, D], BF16, tag="xt")
         gamma_psum = psum_c.tile([P, D], BF16)
         beta_psum = psum_c.tile([P, D], BF16)
         bo_sbuf = consts.tile([P, D], BF16)
@@ -136,7 +138,7 @@ def tile_heterogeneousgraphtransformer_pb_kernel(
                     )
 
             acc_wide = psum_acc.tile([P, N_WIDE], F32)
-            acc_rest = psum_acc.tile([P, D - N_WIDE], F32)
+            acc_rest = psum_acc.tile([P, D - N_WIDE], F32, bufs=1)
             mx_group(acc_wide[:], 0, N_WIDE)
             for n0 in range(N_WIDE, D, N_NARROW):
                 mx_group(acc_rest[:, n0 - N_WIDE : n0 - N_WIDE + N_NARROW], n0, N_NARROW)
@@ -192,23 +194,30 @@ def tile_heterogeneousgraphtransformer_pb_kernel(
         quantise(0, grouped[0])
         nc.vector.tensor_tensor(out=resid[0][:], in0=scene[0][:], in1=bo_psum[:], op=ALU.add)
         for j in range(1, TILES):
-            nc.gpsimd.tensor_tensor(out=resid[j][:], in0=scene[j][:], in1=bo_sbuf[:], op=ALU.add)
-        acc = project(0)
-        grouped[1] = transpose(1)
+            for c0 in range(0, D, RESID_PIECE):
+                piece = slice(c0, c0 + RESID_PIECE)
+                nc.gpsimd.tensor_tensor(
+                    out=resid[j][:, piece], in0=scene[j][:, piece], in1=bo_sbuf[:, piece], op=ALU.add
+                )
+        acc = {0: project(0)}
         spread_vector(1, gamma_psum)
         spread_vector(2, beta_psum)
+        grouped[1] = transpose(1)
 
+        prepared = 1
         previous = None
         for j in range(TILES + 1):
             if j < TILES:
-                y, sums = add_residual(j, *acc)
+                y, sums = add_residual(j, *acc[j])
                 neg_mean, rstd = statistics(y, sums)
-            if j + 2 < TILES:
-                grouped[j + 2] = transpose(j + 2)
-            if j + 1 < TILES:
-                quantise(j + 1, grouped[j + 1])
-                acc = project(j + 1)
             if previous is not None:
                 scale_shift_store(j - 1, *previous)
+            lead = min(j + 1, AHEAD)
+            for t in range(prepared, min(j + 1 + lead, TILES)):
+                if t + 1 < TILES:
+                    grouped[t + 1] = transpose(t + 1)
+                quantise(t, grouped[t])
+                acc[t] = project(t)
+                prepared = t + 1
             if j < TILES:
                 previous = (centre_and_gain(y, neg_mean), rstd)

@@ -193,18 +193,24 @@ def tile_heterogeneousgraphtransformer_pb_kernel(
         nc.scalar.copy(out=bo_sbuf[:], in_=bo_psum[:])
         quantise(0, grouped[0])
         nc.vector.tensor_tensor(out=resid[0][:], in0=scene[0][:], in1=bo_psum[:], op=ALU.add)
-        for j in range(1, TILES):
+
+        seen_words = consts.tile([P, 1], U32)
+        seen_values = consts.tile([P, 1], F32)
+
+        def add_bias_on_gpsimd(j):
             for c0 in range(0, D, RESID_PIECE):
                 piece = slice(c0, c0 + RESID_PIECE)
                 nc.gpsimd.tensor_tensor(
                     out=resid[j][:, piece], in0=scene[j][:, piece], in1=bo_sbuf[:, piece], op=ALU.add
                 )
+
         acc = {0: project(0)}
         spread_vector(1, gamma_psum)
         spread_vector(2, beta_psum)
         grouped[1] = transpose(1)
 
         prepared = 1
+        biased = 1
         previous = None
         for j in range(TILES + 1):
             if j < TILES:
@@ -213,11 +219,21 @@ def tile_heterogeneousgraphtransformer_pb_kernel(
             if previous is not None:
                 scale_shift_store(j - 1, *previous)
             lead = min(j + 1, AHEAD)
+            first = prepared
             for t in range(prepared, min(j + 1 + lead, TILES)):
                 if t + 1 < TILES:
                     grouped[t + 1] = transpose(t + 1)
                 quantise(t, grouped[t])
                 acc[t] = project(t)
                 prepared = t + 1
+            if j == 0:
+                nc.vector.tensor_tensor(out=resid[1][:], in0=scene[1][:], in1=bo_sbuf[:], op=ALU.add)
+                nc.gpsimd.tensor_copy(out=seen_values[:], in_=resid[1][:, D - 1 : D])
+                biased = 2
+            elif prepared > first:
+                nc.gpsimd.tensor_copy(out=seen_words[:], in_=codes[prepared - 1][:, PASSES - 1, P - 1 : P])
+            if prepared > first and biased < TILES:
+                add_bias_on_gpsimd(biased)
+                biased = biased + 1
             if j < TILES:
                 previous = (centre_and_gain(y, neg_mean), rstd)

@@ -23,8 +23,10 @@ PASSES = K // K_PASS
 TILES = S // P
 N_WIDE = 512
 N_NARROW = 128
-RESID_PIECE = 256
+RESID_PIECE = 768
 AHEAD = 2
+HANDED_OVER = (4, 5)
+WARM_UPS = 4
 EPS = 1e-5
 
 FLOPS = 2 * S * K * D
@@ -50,17 +52,19 @@ def tile_heterogeneousgraphtransformer_pb_kernel(
         psum_c = ctx.enter_context(tc.psum_pool(name="psum_c", bufs=1))
         ctx.enter_context(tc.manual_schedule())
 
-        rows = consts.tile([P, 3, D], BF16)
-        nc.vector.memset(rows[:, 0, :].bitcast(I32), 0)
-        w_planes = consts.tile([P, PASSES, D], U8, align_bytes=64)
-        nc.vector.memset(w_planes[:].bitcast(I32), 0)
-        nc.vector.memset(rows[:, 1:3, :].bitcast(I32), 0)
         eps = consts.tile([P, 1], F32)
         nc.vector.memset(eps[:], EPS)
-        ones = consts.tile([P, P], BF16)
-        nc.vector.memset(ones[:], 1.0)
         warm = consts.tile([P, 1], F32)
         nc.scalar.activation(out=warm[:], in_=eps[:], func=ACT.Abs_reciprocal_sqrt)
+        w_planes = consts.tile([P, PASSES, D], U8, align_bytes=64)
+        nc.gpsimd.memset(w_planes[:].bitcast(F32), 0.0)
+        ones = consts.tile([P, P], BF16)
+        nc.gpsimd.memset(ones[:], 1.0)
+        zeros = consts.tile([P, N_WIDE], BF16)
+        nc.gpsimd.memset(zeros[:], 0.0)
+        rows = consts.tile([P, 3, D], BF16)
+        nc.vector.memset(rows[:, 0, :].bitcast(I32), 0)
+        nc.vector.memset(rows[:, 1:3, :].bitcast(I32), 0)
         ident = consts.tile([P, P], F32)
         make_identity(nc, ident[:])
 
@@ -69,16 +73,16 @@ def tile_heterogeneousgraphtransformer_pb_kernel(
         w_words = consts.tile([P, PASSES, 2 * D], U8, align_bytes=64)
 
         nc.sync.dma_start(out=cat[0][:], in_=att_v[0])
-        nc.sync.dma_start(out=rows[0:1, 0, :], in_=bo.unsqueeze(0))
-        nc.sync.dma_start(out=scene[0][:], in_=scene_v[0])
+        nc.sync.dma_start(
+            out=w_words[:].bitcast(I32), in_=Wo_words.bitcast(I32).rearrange("g p n -> p g n")
+        )
         for r in range(4):
             nc.sync.dma_start(
                 out=w_planes[r:P:32].bitcast(I32),
                 in_=Wo_scales.bitcast(I32)[:, r:16:4, :].rearrange("g q n -> q g n"),
             )
-        nc.sync.dma_start(
-            out=w_words[:].bitcast(I32), in_=Wo_words.bitcast(I32).rearrange("g p n -> p g n")
-        )
+        nc.sync.dma_start(out=rows[0:1, 0, :], in_=bo.unsqueeze(0))
+        nc.sync.dma_start(out=scene[0][:], in_=scene_v[0])
         nc.sync.dma_start(out=rows[0:1, 1, :], in_=gamma.unsqueeze(0))
         nc.sync.dma_start(out=rows[0:1, 2, :], in_=beta.unsqueeze(0))
         for j in range(1, TILES):
@@ -188,11 +192,25 @@ def tile_heterogeneousgraphtransformer_pb_kernel(
             )
             nc.sync.dma_start(out=out_v[j], in_=result[:])
 
+        beta_sbuf = consts.tile([P, D], BF16)
+
+        def scale_on_scalar(centred, rstd):
+            scaled = work.tile([P, D], F32)
+            nc.scalar.activation(out=scaled[:], in_=centred[:], func=ACT.Copy, scale=rstd[:])
+            return scaled
+
+        def shift_store_on_gpsimd(j, scaled):
+            shifted = work.tile([P, D], F32)
+            nc.gpsimd.tensor_tensor(out=shifted[:], in0=scaled[:], in1=beta_sbuf[:], op=ALU.add)
+            nc.sync.dma_start(out=out_v[j], in_=shifted[:])
+
+        for i in range(WARM_UPS):
+            nc.tensor.matmul(out=gamma_psum[:, 0:N_WIDE], lhsT=ones[:], rhs=zeros[:], start=True, stop=True)
         grouped = {0: transpose(0)}
         spread_vector(0, bo_psum)
-        nc.scalar.copy(out=bo_sbuf[:], in_=bo_psum[:])
         quantise(0, grouped[0])
         nc.vector.tensor_tensor(out=resid[0][:], in0=scene[0][:], in1=bo_psum[:], op=ALU.add)
+        nc.scalar.copy(out=bo_sbuf[:], in_=bo_psum[:])
 
         seen_words = consts.tile([P, 1], U32)
         seen_values = consts.tile([P, 1], F32)
@@ -212,14 +230,16 @@ def tile_heterogeneousgraphtransformer_pb_kernel(
         prepared = 1
         biased = 1
         previous = None
-        for j in range(TILES + 1):
-            if j < TILES:
-                y, sums = add_residual(j, *acc[j])
-                neg_mean, rstd = statistics(y, sums)
-            if previous is not None:
+        for j in range(TILES - AHEAD):
+            y, sums = add_residual(j, *acc[j])
+            if j - 1 in HANDED_OVER:
+                scaled = scale_on_scalar(*previous)
+            neg_mean, rstd = statistics(y, sums)
+            if previous is not None and j - 1 not in HANDED_OVER:
                 scale_shift_store(j - 1, *previous)
+            if j + 1 == HANDED_OVER[0]:
+                nc.scalar.copy(out=beta_sbuf[:], in_=beta_psum[:])
             lead = min(j + 1, AHEAD)
-            first = prepared
             for t in range(prepared, min(j + 1 + lead, TILES)):
                 if t + 1 < TILES:
                     grouped[t + 1] = transpose(t + 1)
@@ -230,10 +250,22 @@ def tile_heterogeneousgraphtransformer_pb_kernel(
                 nc.vector.tensor_tensor(out=resid[1][:], in0=scene[1][:], in1=bo_sbuf[:], op=ALU.add)
                 nc.gpsimd.tensor_copy(out=seen_values[:], in_=resid[1][:, D - 1 : D])
                 biased = 2
-            elif prepared > first:
+            else:
                 nc.gpsimd.tensor_copy(out=seen_words[:], in_=codes[prepared - 1][:, PASSES - 1, P - 1 : P])
-            if prepared > first and biased < TILES:
-                add_bias_on_gpsimd(biased)
-                biased = biased + 1
-            if j < TILES:
-                previous = (centre_and_gain(y, neg_mean), rstd)
+            add_bias_on_gpsimd(biased)
+            biased = biased + 1
+            if j - 1 in HANDED_OVER:
+                shift_store_on_gpsimd(j - 1, scaled)
+            previous = (centre_and_gain(y, neg_mean), rstd)
+
+        j = TILES - AHEAD
+        y_a, sums_a = add_residual(j, *acc[j])
+        scaled = scale_on_scalar(*previous)
+        neg_mean_a, rstd_a = statistics(y_a, sums_a)
+        shift_store_on_gpsimd(j - 1, scaled)
+        y_b, sums_b = add_residual(j + 1, *acc[j + 1])
+        neg_mean_b, rstd_b = statistics(y_b, sums_b)
+        centred_a = centre_and_gain(y_a, neg_mean_a)
+        centred_b = centre_and_gain(y_b, neg_mean_b)
+        scale_shift_store(j, centred_a, rstd_a)
+        scale_shift_store(j + 1, centred_b, rstd_b)

@@ -25,7 +25,7 @@ N_WIDE = 512
 N_NARROW = 128
 RESID_PIECE = 768
 AHEAD = 2
-HANDED_OVER = (4, 5)
+HANDED_OVER = (4,)
 WARM_UPS = 4
 EPS = 1e-5
 
@@ -213,7 +213,6 @@ def tile_heterogeneousgraphtransformer_pb_kernel(
         nc.scalar.copy(out=bo_sbuf[:], in_=bo_psum[:])
 
         seen_words = consts.tile([P, 1], U32)
-        seen_values = consts.tile([P, 1], F32)
 
         def add_bias_on_gpsimd(j):
             for c0 in range(0, D, RESID_PIECE):
@@ -223,35 +222,38 @@ def tile_heterogeneousgraphtransformer_pb_kernel(
                 )
 
         acc = {0: project(0)}
-        spread_vector(1, gamma_psum)
-        spread_vector(2, beta_psum)
         grouped[1] = transpose(1)
+        spread_vector(1, gamma_psum)
 
         prepared = 1
         biased = 1
         previous = None
         for j in range(TILES - AHEAD):
             y, sums = add_residual(j, *acc[j])
+            neg_mean, rstd = statistics(y, sums)
             if j - 1 in HANDED_OVER:
                 scaled = scale_on_scalar(*previous)
-            neg_mean, rstd = statistics(y, sums)
             if previous is not None and j - 1 not in HANDED_OVER:
                 scale_shift_store(j - 1, *previous)
             if j + 1 == HANDED_OVER[0]:
                 nc.scalar.copy(out=beta_sbuf[:], in_=beta_psum[:])
             lead = min(j + 1, AHEAD)
+            if j == 0:
+                nc.vector.tensor_tensor(out=resid[1][:], in0=scene[1][:], in1=bo_sbuf[:], op=ALU.add)
+                biased = 2
+                quantise(1, grouped[1])
+                acc[1] = project(1)
+                spread_vector(2, beta_psum)
+                grouped[2] = transpose(2)
+                grouped[3] = transpose(3)
+                prepared = 2
             for t in range(prepared, min(j + 1 + lead, TILES)):
-                if t + 1 < TILES:
+                if t + 1 < TILES and t + 1 not in grouped:
                     grouped[t + 1] = transpose(t + 1)
                 quantise(t, grouped[t])
                 acc[t] = project(t)
                 prepared = t + 1
-            if j == 0:
-                nc.vector.tensor_tensor(out=resid[1][:], in0=scene[1][:], in1=bo_sbuf[:], op=ALU.add)
-                nc.gpsimd.tensor_copy(out=seen_values[:], in_=resid[1][:, D - 1 : D])
-                biased = 2
-            else:
-                nc.gpsimd.tensor_copy(out=seen_words[:], in_=codes[prepared - 1][:, PASSES - 1, P - 1 : P])
+            nc.gpsimd.tensor_copy(out=seen_words[:], in_=codes[prepared - 1][:, PASSES - 1, P - 1 : P])
             add_bias_on_gpsimd(biased)
             biased = biased + 1
             if j - 1 in HANDED_OVER:
@@ -260,9 +262,8 @@ def tile_heterogeneousgraphtransformer_pb_kernel(
 
         j = TILES - AHEAD
         y_a, sums_a = add_residual(j, *acc[j])
-        scaled = scale_on_scalar(*previous)
         neg_mean_a, rstd_a = statistics(y_a, sums_a)
-        shift_store_on_gpsimd(j - 1, scaled)
+        scale_shift_store(j - 1, *previous)
         y_b, sums_b = add_residual(j + 1, *acc[j + 1])
         neg_mean_b, rstd_b = statistics(y_b, sums_b)
         centred_a = centre_and_gain(y_a, neg_mean_a)

@@ -37,9 +37,9 @@ def tile_heterogeneousgraphtransformer_pb_kernel(
 ):
     nc = tc.nc
 
-    att_v = att.rearrange("e b (p j) d -> (b j) p e d", j=TILES)
-    scene_v = scene_reps.rearrange("b (p j) d -> (b j) p d", j=TILES)
-    out_v = out.rearrange("b (p j) d -> (b j) p d", j=TILES)
+    att_v = att.rearrange("e b (j p) d -> (b j) p e d", j=TILES)
+    scene_v = scene_reps.rearrange("b (j p) d -> (b j) p d", j=TILES)
+    out_v = out.rearrange("b (j p) d -> (b j) p d", j=TILES)
 
     with ExitStack() as ctx:
         consts = ctx.enter_context(tc.tile_pool(name="consts", bufs=1))

@@ -83,10 +83,11 @@ def tile_heterogeneousgraphtransformer_pb_kernel(
             )
         nc.sync.dma_start(out=rows[0:1, 0, :], in_=bo.unsqueeze(0))
         nc.sync.dma_start(out=scene[0][:], in_=scene_v[0])
-        nc.sync.dma_start(out=rows[0:1, 1, :], in_=gamma.unsqueeze(0))
-        nc.sync.dma_start(out=rows[0:1, 2, :], in_=beta.unsqueeze(0))
         for j in range(1, TILES):
             nc.sync.dma_start(out=cat[j][:], in_=att_v[j])
+            if j == 1:
+                nc.sync.dma_start(out=rows[0:1, 1, :], in_=gamma.unsqueeze(0))
+                nc.sync.dma_start(out=rows[0:1, 2, :], in_=beta.unsqueeze(0))
             nc.sync.dma_start(out=scene[j][:], in_=scene_v[j])
 
         codes = [inputs.tile([P, PASSES, P], U32, name="codes%d" % j, align_bytes=64) for j in range(TILES)]

@@ -28,6 +28,7 @@ AHEAD = 2
 HANDED_OVER = (4,)
 WARM_UPS = 4
 EPS = 1e-5
+TWO_ONES = 0x3F803F80
 
 FLOPS = 2 * S * K * D
 
@@ -52,18 +53,17 @@ def tile_heterogeneousgraphtransformer_pb_kernel(
         psum_c = ctx.enter_context(tc.psum_pool(name="psum_c", bufs=1))
         ctx.enter_context(tc.manual_schedule())
 
+        rows = consts.tile([P, 3, D], BF16)
+        nc.vector.memset(rows[:, 0, :].bitcast(I32), 0)
+        ones_wide = consts.tile([P, N_WIDE], BF16)
+        nc.vector.memset(ones_wide[:].bitcast(I32), TWO_ONES)
+        ones = ones_wide[:, 0:P]
         eps = consts.tile([P, 1], F32)
         nc.vector.memset(eps[:], EPS)
         warm = consts.tile([P, 1], F32)
         nc.scalar.activation(out=warm[:], in_=eps[:], func=ACT.Abs_reciprocal_sqrt)
         w_planes = consts.tile([P, PASSES, D], U8, align_bytes=64)
         nc.gpsimd.memset(w_planes[:].bitcast(F32), 0.0)
-        ones = consts.tile([P, P], BF16)
-        nc.gpsimd.memset(ones[:], 1.0)
-        zeros = consts.tile([P, N_WIDE], BF16)
-        nc.gpsimd.memset(zeros[:], 0.0)
-        rows = consts.tile([P, 3, D], BF16)
-        nc.vector.memset(rows[:, 0, :].bitcast(I32), 0)
         nc.vector.memset(rows[:, 1:3, :].bitcast(I32), 0)
         ident = consts.tile([P, P], F32)
         make_identity(nc, ident[:])
@@ -73,6 +73,7 @@ def tile_heterogeneousgraphtransformer_pb_kernel(
         w_words = consts.tile([P, PASSES, 2 * D], U8, align_bytes=64)
 
         nc.sync.dma_start(out=cat[0][:], in_=att_v[0])
+        nc.sync.dma_start(out=rows[0:1, 0, :], in_=bo.unsqueeze(0))
         nc.sync.dma_start(
             out=w_words[:].bitcast(I32), in_=Wo_words.bitcast(I32).rearrange("g p n -> p g n")
         )
@@ -81,19 +82,19 @@ def tile_heterogeneousgraphtransformer_pb_kernel(
                 out=w_planes[r:P:32].bitcast(I32),
                 in_=Wo_scales.bitcast(I32)[:, r:16:4, :].rearrange("g q n -> q g n"),
             )
-        nc.sync.dma_start(out=rows[0:1, 0, :], in_=bo.unsqueeze(0))
         nc.sync.dma_start(out=scene[0][:], in_=scene_v[0])
-        for j in range(1, TILES):
+        nc.sync.dma_start(out=scene[1][:], in_=scene_v[1])
+        nc.sync.dma_start(out=cat[1][:], in_=att_v[1])
+        nc.sync.dma_start(out=rows[0:1, 1, :], in_=gamma.unsqueeze(0))
+        nc.sync.dma_start(out=rows[0:1, 2, :], in_=beta.unsqueeze(0))
+        for j in range(2, TILES):
             nc.sync.dma_start(out=cat[j][:], in_=att_v[j])
-            if j == 1:
-                nc.sync.dma_start(out=rows[0:1, 1, :], in_=gamma.unsqueeze(0))
-                nc.sync.dma_start(out=rows[0:1, 2, :], in_=beta.unsqueeze(0))
             nc.sync.dma_start(out=scene[j][:], in_=scene_v[j])
 
         codes = [inputs.tile([P, PASSES, P], U32, name="codes%d" % j, align_bytes=64) for j in range(TILES)]
         planes = [inputs.tile([P, PASSES, P], U8, name="planes%d" % j, align_bytes=64) for j in range(TILES)]
         resid = [inputs.tile([P, D], F32, name="resid%d" % j) for j in range(TILES)]
-        bo_psum = psum_t.tile([P, D], BF16, tag="xt")
+        bo_psum = psum_acc.tile([P, D], BF16, tag="acc_wide")
         gamma_psum = psum_c.tile([P, D], BF16)
         beta_psum = psum_c.tile([P, D], BF16)
         bo_sbuf = consts.tile([P, D], BF16)
@@ -102,12 +103,12 @@ def tile_heterogeneousgraphtransformer_pb_kernel(
             for h in range(2):
                 half = slice(h * (D // 2), (h + 1) * (D // 2))
                 nc.tensor.matmul(
-                    out=everywhere[:, half], lhsT=ones[:], rhs=rows[:, i, half], start=True, stop=True
+                    out=everywhere[:, half], lhsT=ones, rhs=rows[:, i, half], start=True, stop=True
                 )
 
-        def transpose(j):
+        def transposes_only(j):
             words = cat[j][:].rearrange("p e d -> p (e d)").bitcast(F32)
-            grouped = []
+            turned = []
             for g in range(PASSES):
                 xt = psum_t.tile([P, 2, P], F32)
                 for u in range(2):
@@ -116,10 +117,19 @@ def tile_heterogeneousgraphtransformer_pb_kernel(
                         in_=words[:, 2 * P * g + u : 2 * P * (g + 1) : 2],
                         identity=ident[:],
                     )
+                turned.append(xt)
+            return turned
+
+        def copies_only(turned):
+            grouped = []
+            for xt in turned:
                 side_by_side = stage.tile([P, P, 4], BF16, align_bytes=64)
                 nc.scalar.copy(out=side_by_side[:].bitcast(F32), in_=xt[:].rearrange("p u r -> p r u"))
                 grouped.append(side_by_side)
             return grouped
+
+        def transpose(j):
+            return copies_only(transposes_only(j))
 
         def quantise(j, grouped):
             for g in range(PASSES):
@@ -206,7 +216,7 @@ def tile_heterogeneousgraphtransformer_pb_kernel(
             nc.sync.dma_start(out=out_v[j], in_=shifted[:])
 
         for i in range(WARM_UPS):
-            nc.tensor.matmul(out=gamma_psum[:, 0:N_WIDE], lhsT=ones[:], rhs=zeros[:], start=True, stop=True)
+            nc.tensor.matmul(out=gamma_psum[:, 0:N_WIDE], lhsT=ones, rhs=ones_wide[:], start=True, stop=True)
         grouped = {0: transpose(0)}
         spread_vector(0, bo_psum)
         quantise(0, grouped[0])
@@ -225,9 +235,10 @@ def tile_heterogeneousgraphtransformer_pb_kernel(
         acc = {0: project(0)}
         grouped[1] = transpose(1)
         spread_vector(1, gamma_psum)
+        xt_2 = transposes_only(2)
 
         prepared = 1
-        biased = 1
+        biased = 2
         previous = None
         for j in range(TILES - AHEAD):
             y, sums = add_residual(j, *acc[j])
@@ -241,11 +252,10 @@ def tile_heterogeneousgraphtransformer_pb_kernel(
             lead = min(j + 1, AHEAD)
             if j == 0:
                 nc.vector.tensor_tensor(out=resid[1][:], in0=scene[1][:], in1=bo_sbuf[:], op=ALU.add)
-                biased = 2
                 quantise(1, grouped[1])
                 acc[1] = project(1)
                 spread_vector(2, beta_psum)
-                grouped[2] = transpose(2)
+                grouped[2] = copies_only(xt_2)
                 grouped[3] = transpose(3)
                 prepared = 2
             for t in range(prepared, min(j + 1 + lead, TILES)):

@@ -23,9 +23,9 @@ PASSES = K // K_PASS
 TILES = S // P
 N_WIDE = 512
 N_NARROW = 128
-RESID_PIECE = 768
+BIAS_SHARE = 960
 AHEAD = 2
-HANDED_OVER = (4,)
+HANDED_OVER = (4, 5)
 WARM_UPS = 4
 EPS = 1e-5
 TWO_ONES = 0x3F803F80
@@ -223,14 +223,14 @@ def tile_heterogeneousgraphtransformer_pb_kernel(
         nc.vector.tensor_tensor(out=resid[0][:], in0=scene[0][:], in1=bo_psum[:], op=ALU.add)
         nc.scalar.copy(out=bo_sbuf[:], in_=bo_psum[:])
 
-        seen_words = consts.tile([P, 1], U32)
-
-        def add_bias_on_gpsimd(j):
-            for c0 in range(0, D, RESID_PIECE):
-                piece = slice(c0, c0 + RESID_PIECE)
-                nc.gpsimd.tensor_tensor(
-                    out=resid[j][:, piece], in0=scene[j][:, piece], in1=bo_sbuf[:, piece], op=ALU.add
-                )
+        def add_bias_on_gpsimd(first, last):
+            for t in range(2, TILES):
+                c0 = max(first - (t - 2) * D, 0)
+                c1 = min(last - (t - 2) * D, D)
+                if c0 < c1:
+                    nc.gpsimd.tensor_tensor(
+                        out=resid[t][:, c0:c1], in0=scene[t][:, c0:c1], in1=bo_sbuf[:, c0:c1], op=ALU.add
+                    )
 
         acc = {0: project(0)}
         grouped[1] = transpose(1)
@@ -238,13 +238,12 @@ def tile_heterogeneousgraphtransformer_pb_kernel(
         xt_2 = transposes_only(2)
 
         prepared = 1
-        biased = 2
         previous = None
         for j in range(TILES - AHEAD):
-            y, sums = add_residual(j, *acc[j])
-            neg_mean, rstd = statistics(y, sums)
             if j - 1 in HANDED_OVER:
                 scaled = scale_on_scalar(*previous)
+            y, sums = add_residual(j, *acc[j])
+            neg_mean, rstd = statistics(y, sums)
             if previous is not None and j - 1 not in HANDED_OVER:
                 scale_shift_store(j - 1, *previous)
             if j + 1 == HANDED_OVER[0]:
@@ -264,17 +263,17 @@ def tile_heterogeneousgraphtransformer_pb_kernel(
                 quantise(t, grouped[t])
                 acc[t] = project(t)
                 prepared = t + 1
-            nc.gpsimd.tensor_copy(out=seen_words[:], in_=codes[prepared - 1][:, PASSES - 1, P - 1 : P])
-            add_bias_on_gpsimd(biased)
-            biased = biased + 1
+            nc.gpsimd.memset(grouped[prepared - 1][PASSES - 1][:, P - 1, 2:4].bitcast(I32), 0)
+            add_bias_on_gpsimd(BIAS_SHARE * j, BIAS_SHARE * (j + 1))
             if j - 1 in HANDED_OVER:
                 shift_store_on_gpsimd(j - 1, scaled)
             previous = (centre_and_gain(y, neg_mean), rstd)
 
         j = TILES - AHEAD
         y_a, sums_a = add_residual(j, *acc[j])
+        scaled = scale_on_scalar(*previous)
         neg_mean_a, rstd_a = statistics(y_a, sums_a)
-        scale_shift_store(j - 1, *previous)
+        shift_store_on_gpsimd(j - 1, scaled)
         y_b, sums_b = add_residual(j + 1, *acc[j + 1])
         neg_mean_b, rstd_b = statistics(y_b, sums_b)
         centred_a = centre_and_gain(y_a, neg_mean_a)

@@ -153,7 +153,10 @@ def tile_heterogeneousgraphtransformer_pb_kernel(
                     )
 
             acc_wide = psum_acc.tile([P, N_WIDE], F32)
-            acc_rest = psum_acc.tile([P, D - N_WIDE], F32, bufs=1)
+            if j == TILES - 1:
+                acc_rest = psum_t.tile([P, D - N_WIDE], F32, tag="xt")
+            else:
+                acc_rest = psum_acc.tile([P, D - N_WIDE], F32, bufs=1)
             mx_group(acc_wide[:], 0, N_WIDE)
             for n0 in range(N_WIDE, D, N_NARROW):
                 mx_group(acc_rest[:, n0 - N_WIDE : n0 - N_WIDE + N_NARROW], n0, N_NARROW)
@@ -172,28 +175,42 @@ def tile_heterogeneousgraphtransformer_pb_kernel(
             )
             return y, sums
 
-        def statistics(y, sums):
+        def minus_mean(sums):
             parts = small.tile([P, 2], F32)
             neg_mean = small.tile([P, 1], F32)
             nc.scalar.activation(
                 out=parts[:], in_=sums[:], func=ACT.Copy, scale=-1.0 / D, accum_out=neg_mean[:]
             )
+            return neg_mean
+
+        def squared_deviations(y, neg_mean):
             squares = work.tile([P, D], F32)
             ssq = small.tile([P, 1], F32)
             nc.scalar.activation(
                 out=squares[:], in_=y[:], func=ACT.Square, bias=neg_mean[:], scale=1.0, accum_out=ssq[:]
             )
+            return ssq
+
+        def inverse_deviation(ssq):
             rstd = small.tile([P, 1], F32)
             nc.scalar.activation(
                 out=rstd[:], in_=ssq[:], func=ACT.Abs_reciprocal_sqrt, bias=eps[:], scale=1.0 / D
             )
-            return neg_mean, rstd
+            return rstd
+
+        def statistics(y, sums):
+            neg_mean = minus_mean(sums)
+            return neg_mean, inverse_deviation(squared_deviations(y, neg_mean))
+
+        def centre(centred, y, neg_mean, columns):
+            nc.vector.scalar_tensor_tensor(
+                out=centred[:, columns], in0=y[:, columns], scalar=neg_mean[:], in1=gamma_psum[:, columns],
+                op0=ALU.add, op1=ALU.mult,
+            )
 
         def centre_and_gain(y, neg_mean):
             centred = work.tile([P, D], F32)
-            nc.vector.scalar_tensor_tensor(
-                out=centred[:], in0=y[:], scalar=neg_mean[:], in1=gamma_psum[:], op0=ALU.add, op1=ALU.mult
-            )
+            centre(centred, y, neg_mean, slice(0, D))
             return centred
 
         def scale_shift_store(j, centred, rstd):
@@ -272,11 +289,24 @@ def tile_heterogeneousgraphtransformer_pb_kernel(
         j = TILES - AHEAD
         y_a, sums_a = add_residual(j, *acc[j])
         scaled = scale_on_scalar(*previous)
-        neg_mean_a, rstd_a = statistics(y_a, sums_a)
+        neg_mean_a = minus_mean(sums_a)
+        ssq_a = squared_deviations(y_a, neg_mean_a)
         shift_store_on_gpsimd(j - 1, scaled)
         y_b, sums_b = add_residual(j + 1, *acc[j + 1])
-        neg_mean_b, rstd_b = statistics(y_b, sums_b)
+        neg_mean_b = minus_mean(sums_b)
+        rstd_a = inverse_deviation(ssq_a)
+        ssq_b = squared_deviations(y_b, neg_mean_b)
+        rstd_b = inverse_deviation(ssq_b)
+        halves = (slice(0, 384), slice(384, D))
         centred_a = centre_and_gain(y_a, neg_mean_a)
-        centred_b = centre_and_gain(y_b, neg_mean_b)
+        centred_b = work.tile([P, D], F32)
+        centre(centred_b, y_b, neg_mean_b, halves[0])
         scale_shift_store(j, centred_a, rstd_a)
-        scale_shift_store(j + 1, centred_b, rstd_b)
+        centre(centred_b, y_b, neg_mean_b, halves[1])
+        result_b = work.tile([P, D], F32)
+        for half in halves:
+            nc.vector.scalar_tensor_tensor(
+                out=result_b[:, half], in0=centred_b[:, half], scalar=rstd_b[:], in1=beta_psum[:, half],
+                op0=ALU.mult, op1=ALU.add,
+            )
+            nc.sync.dma_start(out=out_v[j + 1][:, half], in_=result_b[:, half])

@@ -74,17 +74,17 @@ def tile_heterogeneousgraphtransformer_pb_kernel(
 
         nc.sync.dma_start(out=cat[0][:], in_=att_v[0])
         nc.sync.dma_start(out=rows[0:1, 0, :], in_=bo.unsqueeze(0))
-        nc.sync.dma_start(
-            out=w_words[:].bitcast(I32), in_=Wo_words.bitcast(I32).rearrange("g p n -> p g n")
-        )
+        nc.sync.dma_start(out=scene[0][:], in_=scene_v[0])
         for r in range(4):
             nc.sync.dma_start(
                 out=w_planes[r:P:32].bitcast(I32),
                 in_=Wo_scales.bitcast(I32)[:, r:16:4, :].rearrange("g q n -> q g n"),
             )
-        nc.sync.dma_start(out=scene[0][:], in_=scene_v[0])
-        nc.sync.dma_start(out=scene[1][:], in_=scene_v[1])
+        nc.sync.dma_start(
+            out=w_words[:].bitcast(I32), in_=Wo_words.bitcast(I32).rearrange("g p n -> p g n")
+        )
         nc.sync.dma_start(out=cat[1][:], in_=att_v[1])
+        nc.sync.dma_start(out=scene[1][:], in_=scene_v[1])
         nc.sync.dma_start(out=rows[0:1, 1, :], in_=gamma.unsqueeze(0))
         nc.sync.dma_start(out=rows[0:1, 2, :], in_=beta.unsqueeze(0))
         for j in range(2, TILES):

@@ -20,6 +20,8 @@ E = 2
 K = E * D
 K_PASS = 4 * P
 PASSES = K // K_PASS
+ONE_BY_ONE = ((0, 1), (1, 1), (2, 1))
+JOINED = ((0, 2), (2, 1))
 TILES = S // P
 N_WIDE = 512
 N_NARROW = 128
@@ -106,25 +108,32 @@ def tile_heterogeneousgraphtransformer_pb_kernel(
                     out=everywhere[:, half], lhsT=ones, rhs=rows[:, i, half], start=True, stop=True
                 )
 
+        def pass_groups(j):
+            return ONE_BY_ONE if j < 2 else JOINED
+
         def transposes_only(j):
             words = cat[j][:].rearrange("p e d -> p (e d)").bitcast(F32)
             turned = []
-            for g in range(PASSES):
-                xt = psum_t.tile([P, 2, P], F32)
-                for u in range(2):
-                    nc.tensor.transpose(
-                        out=xt[:, u, :],
-                        in_=words[:, 2 * P * g + u : 2 * P * (g + 1) : 2],
-                        identity=ident[:],
-                    )
+            for first, count in pass_groups(j):
+                xt = psum_t.tile([P, count, 2, P], F32, tag="xt")
+                for g in range(count):
+                    for u in range(2):
+                        w0 = 2 * P * (first + g)
+                        nc.tensor.transpose(
+                            out=xt[:, g, u, :], in_=words[:, w0 + u : w0 + 2 * P : 2], identity=ident[:]
+                        )
                 turned.append(xt)
             return turned
 
         def copies_only(turned):
             grouped = []
             for xt in turned:
-                side_by_side = stage.tile([P, P, 4], BF16, align_bytes=64)
-                nc.scalar.copy(out=side_by_side[:].bitcast(F32), in_=xt[:].rearrange("p u r -> p r u"))
+                count = xt.shape[1]
+                side_by_side = stage.tile([P, count, P, 4], BF16, align_bytes=64, tag="side%d" % count)
+                nc.scalar.copy(
+                    out=side_by_side[:].bitcast(F32),
+                    in_=xt[:].rearrange("p g u r -> p g r u"),
+                )
                 grouped.append(side_by_side)
             return grouped
 
@@ -132,11 +141,12 @@ def tile_heterogeneousgraphtransformer_pb_kernel(
             return copies_only(transposes_only(j))
 
         def quantise(j, grouped):
-            for g in range(PASSES):
+            for (first, count), side_by_side in zip(pass_groups(j), grouped):
+                part = slice(first, first + count)
                 nc.vector.quantize_mx(
-                    out=codes[j][:, g, :].bitcast(FP8X4),
-                    scales=planes[j][:, g, :],
-                    in_=grouped[g][:].rearrange("p r t -> p (r t)"),
+                    out=codes[j][:, part, :].rearrange("p g r -> p (g r)").bitcast(FP8X4),
+                    scales=planes[j][:, part, :].rearrange("p g r -> p (g r)"),
+                    in_=side_by_side[:].rearrange("p g r t -> p (g r t)"),
                 )
 
         def project(j):
@@ -280,7 +290,7 @@ def tile_heterogeneousgraphtransformer_pb_kernel(
                 quantise(t, grouped[t])
                 acc[t] = project(t)
                 prepared = t + 1
-            nc.gpsimd.memset(grouped[prepared - 1][PASSES - 1][:, P - 1, 2:4].bitcast(I32), 0)
+            nc.gpsimd.memset(grouped[prepared - 1][-1][:, 0, P - 1, 2:4].bitcast(I32), 0)
             add_bias_on_gpsimd(BIAS_SHARE * j, BIAS_SHARE * (j + 1))
             if j - 1 in HANDED_OVER:
                 shift_store_on_gpsimd(j - 1, scaled)

@@ -247,7 +247,8 @@ def tile_heterogeneousgraphtransformer_pb_kernel(
         grouped = {0: transpose(0)}
         spread_vector(0, bo_psum)
         quantise(0, grouped[0])
-        nc.vector.tensor_tensor(out=resid[0][:], in0=scene[0][:], in1=bo_psum[:], op=ALU.add)
+        for part in (slice(0, N_WIDE), slice(N_WIDE, D)):
+            nc.vector.tensor_tensor(out=resid[0][:, part], in0=scene[0][:, part], in1=bo_psum[:, part], op=ALU.add)
         nc.scalar.copy(out=bo_sbuf[:], in_=bo_psum[:])
 
         def add_bias_on_gpsimd(first, last):

from contextlib import ExitStack

import concourse.mybir as mybir
from concourse.masks import make_identity

F32 = mybir.dt.float32
BF16 = mybir.dt.bfloat16
I32 = mybir.dt.int32
U32 = mybir.dt.uint32
U8 = mybir.dt.uint8
FP8X4 = mybir.dt.float8_e4m3fn_x4
FP4X4 = mybir.dt.float4_e2m1fn_x4
ALU = mybir.AluOpType
ACT = mybir.ActivationFunctionType

P = 128
S = 1024
D = 768
E = 2
K = E * D
K_PASS = 4 * P
PASSES = K // K_PASS
ONE_BY_ONE = ((0, 1), (1, 1), (2, 1))
JOINED = ((0, 2), (2, 1))
TILES = S // P
N_WIDE = 512
N_NARROW = 128
BIAS_SHARE = 960
AHEAD = 2
HANDED_OVER = (4, 5)
WARM_UPS = 4
EPS = 1e-5
TWO_ONES = 0x3F803F80

FLOPS = 2 * S * K * D


def tile_heterogeneousgraphtransformer_pb_kernel(
    tc, att, scene_reps, Wo_words, Wo_scales, bo, gamma, beta, out
):
    nc = tc.nc

    att_v = att.rearrange("e b (j p) d -> (b j) p e d", j=TILES)
    scene_v = scene_reps.rearrange("b (j p) d -> (b j) p d", j=TILES)
    out_v = out.rearrange("b (j p) d -> (b j) p d", j=TILES)

    with ExitStack() as ctx:
        consts = ctx.enter_context(tc.tile_pool(name="consts", bufs=1))
        inputs = ctx.enter_context(tc.tile_pool(name="inputs", bufs=1))
        stage = ctx.enter_context(tc.tile_pool(name="stage", bufs=12))
        work = ctx.enter_context(tc.tile_pool(name="work", bufs=3))
        small = ctx.enter_context(tc.tile_pool(name="small", bufs=4))
        psum_t = ctx.enter_context(tc.psum_pool(name="psum_t", bufs=3))
        psum_acc = ctx.enter_context(tc.psum_pool(name="psum_acc", bufs=2))
        psum_c = ctx.enter_context(tc.psum_pool(name="psum_c", bufs=1))
        ctx.enter_context(tc.manual_schedule())

        rows = consts.tile([P, 3, D], BF16)
        nc.vector.memset(rows[:, 0, :].bitcast(I32), 0)
        ones_wide = consts.tile([P, N_WIDE], BF16)
        nc.vector.memset(ones_wide[:].bitcast(I32), TWO_ONES)
        ones = ones_wide[:, 0:P]
        eps = consts.tile([P, 1], F32)
        nc.vector.memset(eps[:], EPS)
        warm = consts.tile([P, 1], F32)
        nc.scalar.activation(out=warm[:], in_=eps[:], func=ACT.Abs_reciprocal_sqrt)
        w_planes = consts.tile([P, PASSES, D], U8, align_bytes=64)
        nc.gpsimd.memset(w_planes[:].bitcast(F32), 0.0)
        nc.vector.memset(rows[:, 1:3, :].bitcast(I32), 0)
        ident = consts.tile([P, P], F32)
        make_identity(nc, ident[:])

        cat = [inputs.tile([P, E, D], BF16, name="cat%d" % j) for j in range(TILES)]
        scene = [inputs.tile([P, D], BF16, name="scene%d" % j) for j in range(TILES)]
        w_words = consts.tile([P, PASSES, 2 * D], U8, align_bytes=64)

        nc.sync.dma_start(out=cat[0][:], in_=att_v[0])
        nc.sync.dma_start(out=rows[0:1, 0, :], in_=bo.unsqueeze(0))
        nc.sync.dma_start(out=scene[0][:], in_=scene_v[0])
        for r in range(4):
            nc.sync.dma_start(
                out=w_planes[r:P:32].bitcast(I32),
                in_=Wo_scales.bitcast(I32)[:, r:16:4, :].rearrange("g q n -> q g n"),
            )
        nc.sync.dma_start(
            out=w_words[:].bitcast(I32), in_=Wo_words.bitcast(I32).rearrange("g p n -> p g n")
        )
        nc.sync.dma_start(out=cat[1][:], in_=att_v[1])
        nc.sync.dma_start(out=scene[1][:], in_=scene_v[1])
        nc.sync.dma_start(out=rows[0:1, 1, :], in_=gamma.unsqueeze(0))
        nc.sync.dma_start(out=rows[0:1, 2, :], in_=beta.unsqueeze(0))
        for j in range(2, TILES):
            nc.sync.dma_start(out=cat[j][:], in_=att_v[j])
            nc.sync.dma_start(out=scene[j][:], in_=scene_v[j])

        codes = [inputs.tile([P, PASSES, P], U32, name="codes%d" % j, align_bytes=64) for j in range(TILES)]
        planes = [inputs.tile([P, PASSES, P], U8, name="planes%d" % j, align_bytes=64) for j in range(TILES)]
        resid = [inputs.tile([P, D], F32, name="resid%d" % j) for j in range(TILES)]
        bo_psum = psum_acc.tile([P, D], BF16, tag="acc_wide")
        gamma_psum = psum_c.tile([P, D], BF16)
        beta_psum = psum_c.tile([P, D], BF16)
        bo_sbuf = consts.tile([P, D], BF16)

        def spread_vector(i, everywhere):
            for h in range(2):
                half = slice(h * (D // 2), (h + 1) * (D // 2))
                nc.tensor.matmul(
                    out=everywhere[:, half], lhsT=ones, rhs=rows[:, i, half], start=True, stop=True
                )

        def pass_groups(j):
            return ONE_BY_ONE if j < 2 else JOINED

        def transposes_only(j):
            words = cat[j][:].rearrange("p e d -> p (e d)").bitcast(F32)
            turned = []
            for first, count in pass_groups(j):
                xt = psum_t.tile([P, count, 2, P], F32, tag="xt")
                for g in range(count):
                    for u in range(2):
                        w0 = 2 * P * (first + g)
                        nc.tensor.transpose(
                            out=xt[:, g, u, :], in_=words[:, w0 + u : w0 + 2 * P : 2], identity=ident[:]
                        )
                turned.append(xt)
            return turned

        def copies_only(turned):
            grouped = []
            for xt in turned:
                count = xt.shape[1]
                side_by_side = stage.tile([P, count, P, 4], BF16, align_bytes=64, tag="side%d" % count)
                nc.scalar.copy(
                    out=side_by_side[:].bitcast(F32),
                    in_=xt[:].rearrange("p g u r -> p g r u"),
                )
                grouped.append(side_by_side)
            return grouped

        def transpose(j):
            return copies_only(transposes_only(j))

        def quantise(j, grouped):
            for (first, count), side_by_side in zip(pass_groups(j), grouped):
                part = slice(first, first + count)
                nc.vector.quantize_mx(
                    out=codes[j][:, part, :].rearrange("p g r -> p (g r)").bitcast(FP8X4),
                    scales=planes[j][:, part, :].rearrange("p g r -> p (g r)"),
                    in_=side_by_side[:].rearrange("p g r t -> p (g r t)"),
                )

        def project(j):
            def mx_group(acc, n0, n):
                for g in range(PASSES):
                    nc.tensor.matmul_mx(
                        out=acc,
                        lhsT=codes[j][:, g, :].bitcast(FP8X4),
                        lhsT_scale=planes[j][:, g, :],
                        rhs=w_words[:, g, 2 * n0 : 2 * (n0 + n)].bitcast(FP4X4),
                        rhs_scale=w_planes[:, g, n0 : n0 + n],
                        start=(g == 0),
                        stop=(g == PASSES - 1),
                    )

            acc_wide = psum_acc.tile([P, N_WIDE], F32)
            if j == TILES - 1:
                acc_rest = psum_t.tile([P, D - N_WIDE], F32, tag="xt")
            else:
                acc_rest = psum_acc.tile([P, D - N_WIDE], F32, bufs=1)
            mx_group(acc_wide[:], 0, N_WIDE)
            for n0 in range(N_WIDE, D, N_NARROW):
                mx_group(acc_rest[:, n0 - N_WIDE : n0 - N_WIDE + N_NARROW], n0, N_NARROW)
            return acc_wide, acc_rest

        def add_residual(j, acc_wide, acc_rest):
            y = work.tile([P, D], F32)
            sums = small.tile([P, 2], F32)
            nc.vector.scalar_tensor_tensor(
                out=y[:, 0:N_WIDE], in0=acc_wide[:], scalar=1.0, in1=resid[j][:, 0:N_WIDE],
                op0=ALU.mult, op1=ALU.add, accum_out=sums[:, 0:1],
            )
            nc.vector.scalar_tensor_tensor(
                out=y[:, N_WIDE:D], in0=acc_rest[:], scalar=1.0, in1=resid[j][:, N_WIDE:D],
                op0=ALU.mult, op1=ALU.add, accum_out=sums[:, 1:2],
            )
            return y, sums

        def minus_mean(sums):
            parts = small.tile([P, 2], F32)
            neg_mean = small.tile([P, 1], F32)
            nc.scalar.activation(
                out=parts[:], in_=sums[:], func=ACT.Copy, scale=-1.0 / D, accum_out=neg_mean[:]
            )
            return neg_mean

        def squared_deviations(y, neg_mean):
            squares = work.tile([P, D], F32)
            ssq = small.tile([P, 1], F32)
            nc.scalar.activation(
                out=squares[:], in_=y[:], func=ACT.Square, bias=neg_mean[:], scale=1.0, accum_out=ssq[:]
            )
            return ssq

        def inverse_deviation(ssq):
            rstd = small.tile([P, 1], F32)
            nc.scalar.activation(
                out=rstd[:], in_=ssq[:], func=ACT.Abs_reciprocal_sqrt, bias=eps[:], scale=1.0 / D
            )
            return rstd

        def statistics(y, sums):
            neg_mean = minus_mean(sums)
            return neg_mean, inverse_deviation(squared_deviations(y, neg_mean))

        def centre(centred, y, neg_mean, columns):
            nc.vector.scalar_tensor_tensor(
                out=centred[:, columns], in0=y[:, columns], scalar=neg_mean[:], in1=gamma_psum[:, columns],
                op0=ALU.add, op1=ALU.mult,
            )

        def centre_and_gain(y, neg_mean):
            centred = work.tile([P, D], F32)
            centre(centred, y, neg_mean, slice(0, D))
            return centred

        def scale_shift_store(j, centred, rstd):
            result = work.tile([P, D], F32)
            nc.vector.scalar_tensor_tensor(
                out=result[:], in0=centred[:], scalar=rstd[:], in1=beta_psum[:], op0=ALU.mult, op1=ALU.add
            )
            nc.sync.dma_start(out=out_v[j], in_=result[:])

        beta_sbuf = consts.tile([P, D], BF16)

        def scale_on_scalar(centred, rstd):
            scaled = work.tile([P, D], F32)
            nc.scalar.activation(out=scaled[:], in_=centred[:], func=ACT.Copy, scale=rstd[:])
            return scaled

        def shift_store_on_gpsimd(j, scaled):
            shifted = work.tile([P, D], F32)
            nc.gpsimd.tensor_tensor(out=shifted[:], in0=scaled[:], in1=beta_sbuf[:], op=ALU.add)
            nc.sync.dma_start(out=out_v[j], in_=shifted[:])

        for i in range(WARM_UPS):
            nc.tensor.matmul(out=gamma_psum[:, 0:N_WIDE], lhsT=ones, rhs=ones_wide[:], start=True, stop=True)
        grouped = {0: transpose(0)}
        spread_vector(0, bo_psum)
        quantise(0, grouped[0])
        for part in (slice(0, N_WIDE), slice(N_WIDE, D)):
            nc.vector.tensor_tensor(out=resid[0][:, part], in0=scene[0][:, part], in1=bo_psum[:, part], op=ALU.add)
        nc.scalar.copy(out=bo_sbuf[:], in_=bo_psum[:])

        def add_bias_on_gpsimd(first, last):
            for t in range(2, TILES):
                c0 = max(first - (t - 2) * D, 0)
                c1 = min(last - (t - 2) * D, D)
                if c0 < c1:
                    nc.gpsimd.tensor_tensor(
                        out=resid[t][:, c0:c1], in0=scene[t][:, c0:c1], in1=bo_sbuf[:, c0:c1], op=ALU.add
                    )

        acc = {0: project(0)}
        grouped[1] = transpose(1)
        spread_vector(1, gamma_psum)
        xt_2 = transposes_only(2)

        prepared = 1
        previous = None
        for j in range(TILES - AHEAD):
            if j - 1 in HANDED_OVER:
                scaled = scale_on_scalar(*previous)
            y, sums = add_residual(j, *acc[j])
            neg_mean, rstd = statistics(y, sums)
            if previous is not None and j - 1 not in HANDED_OVER:
                scale_shift_store(j - 1, *previous)
            if j + 1 == HANDED_OVER[0]:
                nc.scalar.copy(out=beta_sbuf[:], in_=beta_psum[:])
            lead = min(j + 1, AHEAD)
            if j == 0:
                nc.vector.tensor_tensor(out=resid[1][:], in0=scene[1][:], in1=bo_sbuf[:], op=ALU.add)
                quantise(1, grouped[1])
                acc[1] = project(1)
                spread_vector(2, beta_psum)
                grouped[2] = copies_only(xt_2)
                grouped[3] = transpose(3)
                prepared = 2
            for t in range(prepared, min(j + 1 + lead, TILES)):
                if t + 1 < TILES and t + 1 not in grouped:
                    grouped[t + 1] = transpose(t + 1)
                quantise(t, grouped[t])
                acc[t] = project(t)
                prepared = t + 1
            nc.gpsimd.memset(grouped[prepared - 1][-1][:, 0, P - 1, 2:4].bitcast(I32), 0)
            add_bias_on_gpsimd(BIAS_SHARE * j, BIAS_SHARE * (j + 1))
            if j - 1 in HANDED_OVER:
                shift_store_on_gpsimd(j - 1, scaled)
            previous = (centre_and_gain(y, neg_mean), rstd)

        j = TILES - AHEAD
        y_a, sums_a = add_residual(j, *acc[j])
        scaled = scale_on_scalar(*previous)
        neg_mean_a = minus_mean(sums_a)
        ssq_a = squared_deviations(y_a, neg_mean_a)
        shift_store_on_gpsimd(j - 1, scaled)
        y_b, sums_b = add_residual(j + 1, *acc[j + 1])
        neg_mean_b = minus_mean(sums_b)
        rstd_a = inverse_deviation(ssq_a)
        ssq_b = squared_deviations(y_b, neg_mean_b)
        rstd_b = inverse_deviation(ssq_b)
        halves = (slice(0, 384), slice(384, D))
        centred_a = centre_and_gain(y_a, neg_mean_a)
        centred_b = work.tile([P, D], F32)
        centre(centred_b, y_b, neg_mean_b, halves[0])
        scale_shift_store(j, centred_a, rstd_a)
        centre(centred_b, y_b, neg_mean_b, halves[1])
        result_b = work.tile([P, D], F32)
        for half in halves:
            nc.vector.scalar_tensor_tensor(
                out=result_b[:, half], in0=centred_b[:, half], scalar=rstd_b[:], in1=beta_psum[:, half],
                op0=ALU.mult, op1=ALU.add,
            )
            nc.sync.dma_start(out=out_v[j + 1][:, half], in_=result_b[:, half])
